import numpy as np
import ml_dtypes


def mxq(x, axis, fmt="e4m3"):
    dtype, down = {"e4m3": (ml_dtypes.float8_e4m3fn, 7), "e5m2": (ml_dtypes.float8_e5m2, 14)}[fmt]
    v = np.moveaxis(np.asarray(x, np.float32).astype(ml_dtypes.bfloat16).astype(np.float64), axis, -1)
    blocks = v.reshape(v.shape[:-1] + (-1, 32))
    amax = np.abs(blocks).max(-1, keepdims=True)
    byte = np.maximum(np.where(amax > 0, np.frexp(amax)[1] - 1 + 127, 0) - down, 1)
    scale = np.exp2(byte - 127.0)
    codes = (blocks / scale).astype(np.float32).astype(dtype).astype(np.float64)
    return np.moveaxis((codes * scale).reshape(v.shape), -1, axis)


WIDE = False


def mx_kscale(k):
    if not WIDE:
        return np.ones(k)
    levels = np.array([10, -10, 5, -5, 0])
    a = np.random.permutation(np.resize(levels, k // 512 * 4)).reshape(k // 512, 4)
    idx = np.arange(k)
    return np.exp2(a[idx // 512, idx % 128 // 32])


BF16 = ml_dtypes.bfloat16


def bf(x):
    return np.asarray(x, np.float32).astype(BF16)


def f64(x):
    return np.asarray(x).astype(np.float64)


E2M1 = np.array([0.0, 0.5, 1.0, 1.5, 2.0, 3.0, 4.0, 6.0, -0.0, -0.5, -1.0, -1.5, -2.0, -3.0, -4.0, -6.0])


def pack_weight(w, fmt):
    k, n = w.shape
    w = f64(bf(w)).reshape(k // 32, 32, n)
    amax = np.abs(w).max(1)
    if fmt == "e4m3":
        byte = np.frexp(amax)[1] - 1 + 127 - 7
    else:
        mant, ex = np.frexp(amax / 6.0)
        byte = np.where(mant > 0.5, ex, ex - 1) + 127
    byte = np.clip(np.where(amax > 0, byte, 1), 1, 254)
    scaled = (w * np.exp2(127.0 - byte)[:, None, :]).reshape(k, n).astype(np.float32)
    by_word = np.ascontiguousarray(scaled.reshape(k // 512, 128, 4, n).transpose(0, 1, 3, 2))
    if fmt == "e4m3":
        words = by_word.astype(ml_dtypes.float8_e4m3fn).view(np.uint8)
    else:
        c = by_word.astype(ml_dtypes.float4_e2m1fn).view(np.uint8) & 0xF
        words = c[..., 0::2] | (c[..., 1::2] << 4)
    return np.ascontiguousarray(words), np.ascontiguousarray(byte.astype(np.uint8).reshape(k // 512, 16, n))


def unpack_weight(words, scales, fmt):
    g, p, n, _ = words.shape
    if fmt == "e4m3":
        vals = np.ascontiguousarray(words).view(ml_dtypes.float8_e4m3fn).astype(np.float64)
    else:
        nib = np.empty((g, p, n, 4), np.uint8)
        nib[..., 0::2] = words & 0xF
        nib[..., 1::2] = words >> 4
        vals = E2M1[nib]
    vals = vals * np.repeat(np.exp2(scales.astype(np.float64) - 127.0), 8, axis=1)[..., None]
    return vals.transpose(0, 1, 3, 2).reshape(g * 512, n)


N, NB, D = 128, 4096, 4096

INV_SQRT_2PI = 1.0 / np.sqrt(2.0 * np.pi)


def phi(t):
    return INV_SQRT_2PI * np.exp(-0.5 * t * t)


def setup_inputs():
    a = np.log2(mx_kscale(NB))
    u = np.exp2(np.round(1.2 * (a - a.min())))
    g = np.where(u > 1.0, np.where(u == u.max(), 0.25, 0.1), 1.0)
    q_mu = 0.5 + 0.2 * np.random.standard_normal(N)
    q_sigma_sq = 0.01 + 0.1 * np.random.random(N)
    theta = np.stack([q_mu / q_sigma_sq, -0.5 / q_sigma_sq], axis=1)
    basis_mu = np.linspace(0.0, 1.0, NB) + 0.01 * np.random.standard_normal(NB)
    basis_sigma = 0.05 * (1.0 + 0.1 * np.random.standard_normal(NB)) * u
    Bv = np.random.standard_normal((NB, D)) * 0.64 / np.sqrt(NB) * (u * g)[:, None]
    Bv_words, Bv_scales = pack_weight(Bv, "e4m3")
    return {"theta": bf(theta), "basis_mu": bf(basis_mu), "basis_sigma": bf(basis_sigma), "Bv_words": Bv_words, "Bv_scales": Bv_scales}


def reference(theta, basis_mu, basis_sigma, Bv_words, Bv_scales):
    theta, basis_mu, basis_sigma = f64(theta), f64(basis_mu), f64(basis_sigma)
    sigma_sq = -0.5 / theta[:, 1]
    mu = theta[:, 0] * sigma_sq
    s = np.sqrt(basis_sigma[None, :] ** 2 + sigma_sq[:, None])
    r = phi((mu[:, None] - basis_mu[None, :]) / s) / s
    context = mxq(r, 1, "e4m3") @ unpack_weight(Bv_words, Bv_scales, "e4m3")
    return context

@@ -1,0 +1,175 @@
+from contextlib import ExitStack
+import math
+
+import concourse.mybir as mybir
+from concourse.masks import make_identity
+
+FLOPS = 2 * 128 * 4096 * 4096
+
+F32 = mybir.dt.float32
+BF16 = mybir.dt.bfloat16
+I32 = mybir.dt.int32
+U32 = mybir.dt.uint32
+U8 = mybir.dt.uint8
+FP8X4 = mybir.dt.float8_e4m3fn_x4
+ACT = mybir.ActivationFunctionType
+ALU = mybir.AluOpType
+
+P = 128
+D = 4096
+G = 8
+NB = 512
+INV_SQRT_2PI = 1.0 / math.sqrt(2.0 * math.pi)
+
+SPLITS = [[4096], [4096], [4096], [4096], [4096], [2048, 2048], [1024] * 4, [1024] * 4]
+
+
+def tile_longtermattention_w_kernel(tc, theta, basis_mu, basis_sigma, Bv_words, Bv_scales, out):
+    nc = tc.nc
+    with ExitStack() as ctx:
+        const = ctx.enter_context(tc.tile_pool(name="const", bufs=1))
+        wpool = ctx.enter_context(tc.tile_pool(name="wpool", bufs=1))
+        rpool = ctx.enter_context(tc.tile_pool(name="rpool", bufs=1))
+        opool = ctx.enter_context(tc.tile_pool(name="opool", bufs=1))
+        psum = ctx.enter_context(tc.psum_pool(name="psum", bufs=1))
+        ctx.enter_context(tc.manual_schedule())
+
+        xb = const.tile([P, 512], BF16, name="xb")
+        th = const.tile([P, 2], BF16, name="th")
+        ident = const.tile([P, P], F32, name="ident")
+        rec = const.tile([P, 1], F32, name="rec")
+        rep = const.tile([P, 2, P], F32, name="rep")
+        msb = const.tile([P, 2, P], F32, name="msb")
+        bp = const.tile([P, 16, 4], F32, name="bp")
+        bs2 = const.tile([P, 32], F32, name="bs2")
+        planes = [const.tile([P, D], U8, name="planes%d" % h, align_bytes=64) for h in range(2)]
+
+        nc.vector.memset(xb[:], 0.0)
+        for h in range(2):
+            nc.vector.memset(planes[h][:].bitcast(I32), 0)
+        nc.scalar.dma_start(out=th[:], in_=theta)
+        nc.scalar.dma_start(out=xb[0:8, :], in_=basis_mu.rearrange("(g k) -> g k", k=512))
+        nc.scalar.dma_start(out=xb[8:16, :], in_=basis_sigma.rearrange("(g k) -> g k", k=512))
+        make_identity(nc, ident[:])
+
+        wt = {}
+
+        def load_words(g):
+            flat = Bv_words[g].rearrange("p n t -> p (n t)")
+            c0 = 0
+            for i, width in enumerate(SPLITS[g]):
+                w = wpool.tile([P, width], U32, name="w%d_%d" % (g, i), align_bytes=64)
+                nc.sync.dma_start(out=w[:].bitcast(I32), in_=flat[:, 4 * c0 : 4 * (c0 + width)].bitcast(I32))
+                wt[(g, i)] = (w, c0)
+                c0 += width
+
+        def load_scales(h):
+            for q in range(4):
+                nc.sync.dma_start(
+                    out=planes[h][32 * q : 32 * q + 16, :].bitcast(I32),
+                    in_=Bv_scales[4 * h : 4 * h + 4, 4 * q : 4 * q + 4, :].bitcast(I32),
+                )
+
+        load_words(0)
+        load_scales(0)
+        load_scales(1)
+        for g in range(1, G):
+            load_words(g)
+
+        nc.vector.reciprocal(rec[:], th[:, 1:2])
+        nc.vector.tensor_scalar(
+            out=rep[:, 1, :], in0=rec[:, 0:1].to_broadcast([P, P]), scalar1=-0.5, scalar2=None, op0=ALU.mult
+        )
+        nc.vector.scalar_tensor_tensor(
+            out=rep[:, 0, :],
+            in0=rec[:, 0:1].to_broadcast([P, P]),
+            scalar=-0.5,
+            in1=th[:, 0:1].to_broadcast([P, P]),
+            op0=ALU.mult,
+            op1=ALU.mult,
+        )
+        prep = psum.tile([P, 4, P], F32, name="prep", tag="bank7")
+        xw = xb[:].bitcast(F32)
+        for u in range(2):
+            nc.tensor.transpose(prep[:, 2 + u, :], xw[:, u:256:2], ident[:])
+        for m in range(2):
+            nc.tensor.transpose(prep[:, m, :], rep[:, m, :], ident[:])
+        nc.vector.tensor_copy(
+            out=bp[:].rearrange("p r (u e) -> p r u e", e=2),
+            in_=prep[:, 2:4, :].bitcast(BF16).rearrange("p u (r e) -> p r u e", e=2)[:, 0:16],
+        )
+        bm = bp[:, 0:8, :].rearrange("p g t -> p (g t)")
+        bs = bp[:, 8:16, :].rearrange("p g t -> p (g t)")
+        nc.vector.tensor_tensor(out=bs2[:], in0=bs, in1=bs, op=ALU.mult)
+        nc.vector.tensor_copy(out=msb[:], in_=prep[:, 0:2, :])
+
+        inv = [rpool.tile([P, 4, P], F32, name="inv%d" % g) for g in range(G)]
+        zz = [rpool.tile([P, 4, P], F32, name="zz%d" % g) for g in range(G)]
+        rbf = [rpool.tile([P, 4 * P], BF16, name="rbf%d" % g, align_bytes=64) for g in range(G)]
+        rq = [rpool.tile([P, P], U32, name="rq%d" % g, align_bytes=64) for g in range(G)]
+        rs = [rpool.tile([P, P], U8, name="rs%d" % g, align_bytes=64) for g in range(G)]
+
+        for g in range(G):
+            for t in range(4):
+                gt = 4 * g + t
+                nc.scalar.activation(
+                    out=inv[g][:, t, :],
+                    in_=msb[:, 1, :],
+                    func=ACT.Abs_reciprocal_sqrt,
+                    bias=bs2[:, gt : gt + 1],
+                    scale=1.0,
+                )
+                nc.vector.scalar_tensor_tensor(
+                    out=zz[g][:, t, :],
+                    in0=msb[:, 0, :],
+                    scalar=bm[:, gt : gt + 1],
+                    in1=inv[g][:, t, :],
+                    op0=ALU.subtract,
+                    op1=ALU.mult,
+                )
+        for g in range(G):
+            nc.scalar.activation(out=zz[g][:], in_=zz[g][:], func=ACT.Square)
+            nc.scalar.activation(out=zz[g][:], in_=zz[g][:], func=ACT.Exp, scale=-0.5)
+            nc.vector.scalar_tensor_tensor(
+                out=rbf[g][:].rearrange("p (n t) -> p n t", t=4),
+                in0=zz[g][:].rearrange("p t n -> p n t"),
+                scalar=INV_SQRT_2PI,
+                in1=inv[g][:].rearrange("p t n -> p n t"),
+                op0=ALU.mult,
+                op1=ALU.mult,
+            )
+            nc.vector.quantize_mx(out=rq[g][:].bitcast(FP8X4), scales=rs[g][:], in_=rbf[g][:])
+
+        acc = [psum.tile([P, NB], F32, name="acc%d" % c, tag="bank%d" % c) for c in range(D // NB)]
+
+        def passes(g, i):
+            w, c0 = wt[(g, i)]
+            k = 4 * (g % 4)
+            for j in range(SPLITS[g][i] // NB):
+                col = c0 + j * NB
+                nc.tensor.matmul_mx(
+                    out=acc[col // NB][:],
+                    lhsT=rq[g][:].bitcast(FP8X4),
+                    lhsT_scale=rs[g][:],
+                    rhs=w[:, j * NB : (j + 1) * NB].bitcast(FP8X4),
+                    rhs_scale=planes[g // 4][k:P, col : col + NB],
+                    start=(g == 0),
+                    stop=(g == G - 1),
+                )
+
+        for g in range(G - 1):
+            for i in range(len(SPLITS[g])):
+                passes(g, i)
+
+        for i, width in enumerate(SPLITS[G - 1]):
+            passes(G - 1, i)
+            c0 = wt[(G - 1, i)][1]
+            ost = opool.tile([P, width], F32, name="ost%d" % i)
+            for j in range(width // NB):
+                src = acc[c0 // NB + j][:]
+                dst = ost[:, j * NB : (j + 1) * NB]
+                if j % 2 == 0:
+                    nc.scalar.copy(out=dst, in_=src)
+                else:
+                    nc.vector.tensor_copy(out=dst, in_=src)
+            nc.sync.dma_start(out=out[:, c0 : c0 + width], in_=ost[:])

@@ -64,10 +64,10 @@ def tile_longtermattention_w_kernel(tc, theta, basis_mu, basis_sigma, Bv_words, 
                 c0 += width
 
         def load_scales(h):
-            for q in range(4):
-                nc.sync.dma_start(
-                    out=planes[h][32 * q : 32 * q + 16, :].bitcast(I32),
-                    in_=Bv_scales[4 * h : 4 * h + 4, 4 * q : 4 * q + 4, :].bitcast(I32),
+            for q in (0, 2, 1, 3):
+                nc.gpsimd.dma_start(
+                    out=planes[h][32 * q : 32 * q + 16, :].bitcast(F32),
+                    in_=Bv_scales[4 * h : 4 * h + 4, 4 * q : 4 * q + 4, :].bitcast(F32),
                 )
 
         load_words(0)

@@ -21,11 +21,14 @@ G = 8
 NB = 512
 INV_SQRT_2PI = 1.0 / math.sqrt(2.0 * math.pi)
 
-SPLITS = [[4096], [4096], [4096], [4096], [4096], [2048, 2048], [1024] * 4, [1024] * 4]
+TAIL = [1024, 1024, 1024, 512, 512]
+SPLITS = [[4096], [4096], [4096], [4096], [4096], [2048, 2048], TAIL, TAIL]
 
 
 def tile_longtermattention_w_kernel(tc, theta, basis_mu, basis_sigma, Bv_words, Bv_scales, out):
     nc = tc.nc
+    order = [(g, i) for g in range(G - 2) for i in range(len(SPLITS[g]))]
+    order += [(g, i) for i in range(len(TAIL)) for g in (G - 2, G - 1)]
     with ExitStack() as ctx:
         const = ctx.enter_context(tc.tile_pool(name="const", bufs=1))
         wpool = ctx.enter_context(tc.tile_pool(name="wpool", bufs=1))
@@ -54,27 +57,29 @@ def tile_longtermattention_w_kernel(tc, theta, basis_mu, basis_sigma, Bv_words, 
 
         wt = {}
 
-        def load_words(g):
+        def load_words(g, i):
+            c0 = sum(SPLITS[g][:i])
+            width = SPLITS[g][i]
             flat = Bv_words[g].rearrange("p n t -> p (n t)")
-            c0 = 0
-            for i, width in enumerate(SPLITS[g]):
-                w = wpool.tile([P, width], U32, name="w%d_%d" % (g, i), align_bytes=64)
-                nc.sync.dma_start(out=w[:].bitcast(I32), in_=flat[:, 4 * c0 : 4 * (c0 + width)].bitcast(I32))
-                wt[(g, i)] = (w, c0)
-                c0 += width
+            w = wpool.tile([P, width], U32, name="w%d_%d" % (g, i), align_bytes=64)
+            nc.sync.dma_start(out=w[:].bitcast(I32), in_=flat[:, 4 * c0 : 4 * (c0 + width)].bitcast(I32))
+            wt[(g, i)] = (w, c0)
 
         def load_scales(h):
-            for q in (0, 2, 1, 3):
-                nc.gpsimd.dma_start(
-                    out=planes[h][32 * q : 32 * q + 16, :].bitcast(F32),
-                    in_=Bv_scales[4 * h : 4 * h + 4, 4 * q : 4 * q + 4, :].bitcast(F32),
-                )
+            for q in range(4):
+                pieces = 4 if (h == 1 and q == 3) else 1
+                step = D // pieces
+                for c in range(0, D, step):
+                    nc.sync.dma_start(
+                        out=planes[h][32 * q : 32 * q + 16, c : c + step].bitcast(I32),
+                        in_=Bv_scales[4 * h : 4 * h + 4, 4 * q : 4 * q + 4, c : c + step].bitcast(I32),
+                    )
 
-        load_words(0)
+        load_words(0, 0)
         load_scales(0)
         load_scales(1)
-        for g in range(1, G):
-            load_words(g)
+        for g, i in order[1:]:
+            load_words(g, i)
 
         nc.vector.reciprocal(rec[:], th[:, 1:2])
         nc.vector.tensor_scalar(
@@ -142,10 +147,11 @@ def tile_longtermattention_w_kernel(tc, theta, basis_mu, basis_sigma, Bv_words, 
 
         acc = [psum.tile([P, NB], F32, name="acc%d" % c, tag="bank%d" % c) for c in range(D // NB)]
 
-        def passes(g, i):
+        for g, i in order:
             w, c0 = wt[(g, i)]
+            width = SPLITS[g][i]
             k = 4 * (g % 4)
-            for j in range(SPLITS[g][i] // NB):
+            for j in range(width // NB):
                 col = c0 + j * NB
                 nc.tensor.matmul_mx(
                     out=acc[col // NB][:],
@@ -156,20 +162,13 @@ def tile_longtermattention_w_kernel(tc, theta, basis_mu, basis_sigma, Bv_words, 
                     start=(g == 0),
                     stop=(g == G - 1),
                 )
-
-        for g in range(G - 1):
-            for i in range(len(SPLITS[g])):
-                passes(g, i)
-
-        for i, width in enumerate(SPLITS[G - 1]):
-            passes(G - 1, i)
-            c0 = wt[(G - 1, i)][1]
-            ost = opool.tile([P, width], F32, name="ost%d" % i)
-            for j in range(width // NB):
-                src = acc[c0 // NB + j][:]
-                dst = ost[:, j * NB : (j + 1) * NB]
-                if j % 2 == 0:
-                    nc.scalar.copy(out=dst, in_=src)
-                else:
-                    nc.vector.tensor_copy(out=dst, in_=src)
-            nc.sync.dma_start(out=out[:, c0 : c0 + width], in_=ost[:])
+            if g == G - 1:
+                ost = opool.tile([P, width], F32, name="ost%d" % i)
+                for j in range(width // NB):
+                    bank = c0 // NB + j
+                    dst = ost[:, j * NB : (j + 1) * NB]
+                    if bank % 2 == 0:
+                        nc.scalar.copy(out=dst, in_=acc[bank][:])
+                    else:
+                        nc.vector.tensor_copy(out=dst, in_=acc[bank][:])
+                nc.sync.dma_start(out=out[:, c0 : c0 + width], in_=ost[:])

@@ -22,7 +22,7 @@ NB = 512
 INV_SQRT_2PI = 1.0 / math.sqrt(2.0 * math.pi)
 
 TAIL = [1024, 1024, 1024, 512, 512]
-SPLITS = [[4096], [4096], [4096], [4096], [4096], [2048, 2048], TAIL, TAIL]
+SPLITS = [[4096], [4096], [4096], [4096], [4096], [4096], TAIL, TAIL]
 
 
 def tile_longtermattention_w_kernel(tc, theta, basis_mu, basis_sigma, Bv_words, Bv_scales, out):
@@ -67,13 +67,10 @@ def tile_longtermattention_w_kernel(tc, theta, basis_mu, basis_sigma, Bv_words, 
 
         def load_scales(h):
             for q in range(4):
-                pieces = 4 if (h == 1 and q == 3) else 1
-                step = D // pieces
-                for c in range(0, D, step):
-                    nc.sync.dma_start(
-                        out=planes[h][32 * q : 32 * q + 16, c : c + step].bitcast(I32),
-                        in_=Bv_scales[4 * h : 4 * h + 4, 4 * q : 4 * q + 4, c : c + step].bitcast(I32),
-                    )
+                nc.sync.dma_start(
+                    out=planes[h][32 * q : 32 * q + 16, :].bitcast(I32),
+                    in_=Bv_scales[4 * h : 4 * h + 4, 4 * q : 4 * q + 4, :].bitcast(I32),
+                )
 
         load_words(0, 0)
         load_scales(0)

@@ -47,9 +47,9 @@ def tile_longtermattention_w_kernel(tc, theta, basis_mu, basis_sigma, Bv_words, 
         bs2 = const.tile([P, 32], F32, name="bs2")
         planes = [const.tile([P, D], U8, name="planes%d" % h, align_bytes=64) for h in range(2)]
 
+        nc.vector.memset(planes[1][:].bitcast(I32), 0)
         nc.vector.memset(xb[:], 0.0)
-        for h in range(2):
-            nc.vector.memset(planes[h][:].bitcast(I32), 0)
+        nc.vector.memset(planes[0][:].bitcast(I32), 0)
         nc.scalar.dma_start(out=th[:], in_=theta)
         nc.scalar.dma_start(out=xb[0:8, :], in_=basis_mu.rearrange("(g k) -> g k", k=512))
         nc.scalar.dma_start(out=xb[8:16, :], in_=basis_sigma.rearrange("(g k) -> g k", k=512))
@@ -65,16 +65,18 @@ def tile_longtermattention_w_kernel(tc, theta, basis_mu, basis_sigma, Bv_words, 
             nc.sync.dma_start(out=w[:].bitcast(I32), in_=flat[:, 4 * c0 : 4 * (c0 + width)].bitcast(I32))
             wt[(g, i)] = (w, c0)
 
-        def load_scales(h):
-            for q in range(4):
-                nc.sync.dma_start(
-                    out=planes[h][32 * q : 32 * q + 16, :].bitcast(I32),
-                    in_=Bv_scales[4 * h : 4 * h + 4, 4 * q : 4 * q + 4, :].bitcast(I32),
-                )
+        for q in (0, 2, 1, 3):
+            nc.gpsimd.dma_start(
+                out=planes[1][32 * q : 32 * q + 16, :].bitcast(F32),
+                in_=Bv_scales[4:8, 4 * q : 4 * q + 4, :].bitcast(F32),
+            )
 
         load_words(0, 0)
-        load_scales(0)
-        load_scales(1)
+        for q in range(4):
+            nc.sync.dma_start(
+                out=planes[0][32 * q : 32 * q + 16, :].bitcast(I32),
+                in_=Bv_scales[0:4, 4 * q : 4 * q + 4, :].bitcast(I32),
+            )
         for g, i in order[1:]:
             load_words(g, i)
 

from contextlib import ExitStack
import math

import concourse.mybir as mybir
from concourse.masks import make_identity

FLOPS = 2 * 128 * 4096 * 4096

F32 = mybir.dt.float32
BF16 = mybir.dt.bfloat16
I32 = mybir.dt.int32
U32 = mybir.dt.uint32
U8 = mybir.dt.uint8
FP8X4 = mybir.dt.float8_e4m3fn_x4
ACT = mybir.ActivationFunctionType
ALU = mybir.AluOpType

P = 128
D = 4096
G = 8
NB = 512
INV_SQRT_2PI = 1.0 / math.sqrt(2.0 * math.pi)

TAIL = [1024, 1024, 1024, 512, 512]
SPLITS = [[4096], [4096], [4096], [4096], [4096], [4096], TAIL, TAIL]


def tile_longtermattention_w_kernel(tc, theta, basis_mu, basis_sigma, Bv_words, Bv_scales, out):
    nc = tc.nc
    order = [(g, i) for g in range(G - 2) for i in range(len(SPLITS[g]))]
    order += [(g, i) for i in range(len(TAIL)) for g in (G - 2, G - 1)]
    with ExitStack() as ctx:
        const = ctx.enter_context(tc.tile_pool(name="const", bufs=1))
        wpool = ctx.enter_context(tc.tile_pool(name="wpool", bufs=1))
        rpool = ctx.enter_context(tc.tile_pool(name="rpool", bufs=1))
        opool = ctx.enter_context(tc.tile_pool(name="opool", bufs=1))
        psum = ctx.enter_context(tc.psum_pool(name="psum", bufs=1))
        ctx.enter_context(tc.manual_schedule())

        xb = const.tile([P, 512], BF16, name="xb")
        th = const.tile([P, 2], BF16, name="th")
        ident = const.tile([P, P], F32, name="ident")
        rec = const.tile([P, 1], F32, name="rec")
        rep = const.tile([P, 2, P], F32, name="rep")
        msb = const.tile([P, 2, P], F32, name="msb")
        bp = const.tile([P, 16, 4], F32, name="bp")
        bs2 = const.tile([P, 32], F32, name="bs2")
        planes = [const.tile([P, D], U8, name="planes%d" % h, align_bytes=64) for h in range(2)]

        nc.vector.memset(planes[1][:].bitcast(I32), 0)
        nc.vector.memset(xb[:], 0.0)
        nc.vector.memset(planes[0][:].bitcast(I32), 0)
        nc.scalar.dma_start(out=th[:], in_=theta)
        nc.scalar.dma_start(out=xb[0:8, :], in_=basis_mu.rearrange("(g k) -> g k", k=512))
        nc.scalar.dma_start(out=xb[8:16, :], in_=basis_sigma.rearrange("(g k) -> g k", k=512))
        make_identity(nc, ident[:])

        wt = {}

        def load_words(g, i):
            c0 = sum(SPLITS[g][:i])
            width = SPLITS[g][i]
            flat = Bv_words[g].rearrange("p n t -> p (n t)")
            w = wpool.tile([P, width], U32, name="w%d_%d" % (g, i), align_bytes=64)
            nc.sync.dma_start(out=w[:].bitcast(I32), in_=flat[:, 4 * c0 : 4 * (c0 + width)].bitcast(I32))
            wt[(g, i)] = (w, c0)

        for q in (0, 2, 1, 3):
            nc.gpsimd.dma_start(
                out=planes[1][32 * q : 32 * q + 16, :].bitcast(F32),
                in_=Bv_scales[4:8, 4 * q : 4 * q + 4, :].bitcast(F32),
            )

        load_words(0, 0)
        for q in range(4):
            nc.sync.dma_start(
                out=planes[0][32 * q : 32 * q + 16, :].bitcast(I32),
                in_=Bv_scales[0:4, 4 * q : 4 * q + 4, :].bitcast(I32),
            )
        for g, i in order[1:]:
            load_words(g, i)

        nc.vector.reciprocal(rec[:], th[:, 1:2])
        nc.vector.tensor_scalar(
            out=rep[:, 1, :], in0=rec[:, 0:1].to_broadcast([P, P]), scalar1=-0.5, scalar2=None, op0=ALU.mult
        )
        nc.vector.scalar_tensor_tensor(
            out=rep[:, 0, :],
            in0=rec[:, 0:1].to_broadcast([P, P]),
            scalar=-0.5,
            in1=th[:, 0:1].to_broadcast([P, P]),
            op0=ALU.mult,
            op1=ALU.mult,
        )
        prep = psum.tile([P, 4, P], F32, name="prep", tag="bank7")
        xw = xb[:].bitcast(F32)
        for u in range(2):
            nc.tensor.transpose(prep[:, 2 + u, :], xw[:, u:256:2], ident[:])
        for m in range(2):
            nc.tensor.transpose(prep[:, m, :], rep[:, m, :], ident[:])
        nc.vector.tensor_copy(
            out=bp[:].rearrange("p r (u e) -> p r u e", e=2),
            in_=prep[:, 2:4, :].bitcast(BF16).rearrange("p u (r e) -> p r u e", e=2)[:, 0:16],
        )
        bm = bp[:, 0:8, :].rearrange("p g t -> p (g t)")
        bs = bp[:, 8:16, :].rearrange("p g t -> p (g t)")
        nc.vector.tensor_tensor(out=bs2[:], in0=bs, in1=bs, op=ALU.mult)
        nc.vector.tensor_copy(out=msb[:], in_=prep[:, 0:2, :])

        inv = [rpool.tile([P, 4, P], F32, name="inv%d" % g) for g in range(G)]
        zz = [rpool.tile([P, 4, P], F32, name="zz%d" % g) for g in range(G)]
        rbf = [rpool.tile([P, 4 * P], BF16, name="rbf%d" % g, align_bytes=64) for g in range(G)]
        rq = [rpool.tile([P, P], U32, name="rq%d" % g, align_bytes=64) for g in range(G)]
        rs = [rpool.tile([P, P], U8, name="rs%d" % g, align_bytes=64) for g in range(G)]

        for g in range(G):
            for t in range(4):
                gt = 4 * g + t
                nc.scalar.activation(
                    out=inv[g][:, t, :],
                    in_=msb[:, 1, :],
                    func=ACT.Abs_reciprocal_sqrt,
                    bias=bs2[:, gt : gt + 1],
                    scale=1.0,
                )
                nc.vector.scalar_tensor_tensor(
                    out=zz[g][:, t, :],
                    in0=msb[:, 0, :],
                    scalar=bm[:, gt : gt + 1],
                    in1=inv[g][:, t, :],
                    op0=ALU.subtract,
                    op1=ALU.mult,
                )
        for g in range(G):
            nc.scalar.activation(out=zz[g][:], in_=zz[g][:], func=ACT.Square)
            nc.scalar.activation(out=zz[g][:], in_=zz[g][:], func=ACT.Exp, scale=-0.5)
            nc.vector.scalar_tensor_tensor(
                out=rbf[g][:].rearrange("p (n t) -> p n t", t=4),
                in0=zz[g][:].rearrange("p t n -> p n t"),
                scalar=INV_SQRT_2PI,
                in1=inv[g][:].rearrange("p t n -> p n t"),
                op0=ALU.mult,
                op1=ALU.mult,
            )
            nc.vector.quantize_mx(out=rq[g][:].bitcast(FP8X4), scales=rs[g][:], in_=rbf[g][:])

        acc = [psum.tile([P, NB], F32, name="acc%d" % c, tag="bank%d" % c) for c in range(D // NB)]

        for g, i in order:
            w, c0 = wt[(g, i)]
            width = SPLITS[g][i]
            k = 4 * (g % 4)
            for j in range(width // NB):
                col = c0 + j * NB
                nc.tensor.matmul_mx(
                    out=acc[col // NB][:],
                    lhsT=rq[g][:].bitcast(FP8X4),
                    lhsT_scale=rs[g][:],
                    rhs=w[:, j * NB : (j + 1) * NB].bitcast(FP8X4),
                    rhs_scale=planes[g // 4][k:P, col : col + NB],
                    start=(g == 0),
                    stop=(g == G - 1),
                )
            if g == G - 1:
                ost = opool.tile([P, width], F32, name="ost%d" % i)
                for j in range(width // NB):
                    bank = c0 // NB + j
                    dst = ost[:, j * NB : (j + 1) * NB]
                    if bank % 2 == 0:
                        nc.scalar.copy(out=dst, in_=acc[bank][:])
                    else:
                        nc.vector.tensor_copy(out=dst, in_=acc[bank][:])
                nc.sync.dma_start(out=out[:, c0 : c0 + width], in_=ost[:])
